import numpy as np
import ml_dtypes


def mxq(x, axis, fmt="e4m3"):
    dtype, down = {"e4m3": (ml_dtypes.float8_e4m3fn, 7), "e5m2": (ml_dtypes.float8_e5m2, 14)}[fmt]
    v = np.moveaxis(np.asarray(x, np.float32).astype(ml_dtypes.bfloat16).astype(np.float64), axis, -1)
    blocks = v.reshape(v.shape[:-1] + (-1, 32))
    amax = np.abs(blocks).max(-1, keepdims=True)
    byte = np.maximum(np.where(amax > 0, np.frexp(amax)[1] - 1 + 127, 0) - down, 1)
    scale = np.exp2(byte - 127.0)
    codes = (blocks / scale).astype(np.float32).astype(dtype).astype(np.float64)
    return np.moveaxis((codes * scale).reshape(v.shape), -1, axis)


WIDE = False


def mx_kscale(k):
    if not WIDE:
        return np.ones(k)
    levels = np.array([10, -10, 5, -5, 0])
    if k % 512:
        return np.exp2(np.random.permutation(np.resize(levels, k // 32))).repeat(32)
    a = np.empty((k // 512, 16))
    for p in range(k // 512):
        a[p, :8] = np.random.permutation(np.resize(levels, 8))
        for g in range(8):
            far = levels[np.abs(levels - a[p, g]) >= 10]
            a[p, g + 8] = far[np.random.randint(len(far))]
    return np.exp2(a.ravel()).repeat(32)


BF16 = ml_dtypes.bfloat16


def bf(x):
    return np.asarray(x, np.float32).astype(BF16)


def f64(x):
    return np.asarray(x).astype(np.float64)


B, N, D, H, DK, P = 4, 2048, 512, 2, 128, 512
E = H * DK


def draw0():
    s = mx_kscale(D)
    return {"Q": bf(np.random.standard_normal((B, N, D)) * s),
            "WQ": bf(np.random.standard_normal((E, D)) * 1.5 / np.sqrt(D) / s)}


def core(Q, WQ):
    q = mxq(f64(Q), 2, "e4m3") @ mxq(f64(WQ), 1, "e4m3").T
    q = q.reshape(B, N, H, DK).transpose(0, 2, 1, 3)
    g = np.exp(q - q.max(-1, keepdims=True))
    return g / g.sum(-1, keepdims=True)


def e4m3fn_bytes(y):
    return np.clip(np.asarray(y, np.float64), -448.0, 448.0).astype(np.float32).astype(ml_dtypes.float8_e4m3fn).view(np.uint8)


def e4m3fn_values(b):
    return np.asarray(b, np.uint8).view(ml_dtypes.float8_e4m3fn).astype(np.float64)


def setup_inputs():
    d = draw0()
    x0 = np.asarray(d['Q']).astype(np.float64)
    s = (np.max(np.abs(x0), axis=(0, 1), keepdims=True) / 448.0).astype(np.float32)
    out = {}
    for k, v in d.items():
        if k == 'Q':
            out['Q_bytes'] = e4m3fn_bytes(x0 / s.astype(np.float64))
            out['Q_scale'] = s
        else:
            out[k] = v
    return out


def reference(Q_bytes, Q_scale, WQ):
    return core(e4m3fn_values(Q_bytes) * Q_scale.astype(np.float64), WQ)

@@ -1,0 +1,287 @@
+from contextlib import ExitStack
+
+import concourse.mybir as mybir
+from concourse.masks import make_identity
+
+FLOPS = 2 * 8192 * 512 * 256
+
+F32 = mybir.dt.float32
+BF16 = mybir.dt.bfloat16
+U32 = mybir.dt.uint32
+U8 = mybir.dt.uint8
+FP8 = mybir.dt.float8_e4m3fn
+FP8X4 = mybir.dt.float8_e4m3fn_x4
+ACT = mybir.ActivationFunctionType
+ALU = mybir.AluOpType
+AX = mybir.AxisListType
+
+P = 128
+K = 512
+BATCH = 4
+HEADS = 2
+DK = 128
+LOADS = 16
+UNITS = 32
+UW = 2 * K
+
+GROUPS = (
+    [[u] for u in range(4)]
+    + [[u, u + 1] for u in range(4, UNITS - 2, 2)]
+    + [[UNITS - 2], [UNITS - 1]]
+)
+POOL_SHARE = {1: (3,), 2: (0, 5)}
+TAIL_GROUPS = 5
+TAIL_VECTOR = (1, 2, 4, 5, 7)
+WARM_MATMULS = 4
+
+
+def tile_multiheadattention_pb_t_kernel(tc, Q_bytes, Q_scale, WQ, out):
+    nc = tc.nc
+    n_groups = len(GROUPS)
+    with ExitStack() as ctx:
+        const = ctx.enter_context(tc.tile_pool(name="const", bufs=1))
+        bytes_pool = ctx.enter_context(tc.tile_pool(name="bytes_pool", bufs=LOADS))
+        xb_pool = ctx.enter_context(tc.tile_pool(name="xb_pool", bufs=3))
+        g_pool = ctx.enter_context(tc.tile_pool(name="g_pool", bufs=3))
+        c_pool = ctx.enter_context(tc.tile_pool(name="c_pool", bufs=3))
+        st_pool = ctx.enter_context(tc.tile_pool(name="st_pool", bufs=5))
+        e_pool = ctx.enter_context(tc.tile_pool(name="e_pool", bufs=8))
+        o_pool = ctx.enter_context(tc.tile_pool(name="o_pool", bufs=8))
+        tp_pool = ctx.enter_context(tc.psum_pool(name="tp_pool", bufs=4))
+        qp_pool = ctx.enter_context(tc.psum_pool(name="qp_pool", bufs=4))
+        ctx.enter_context(tc.manual_schedule())
+
+        sc4 = const.tile([P, 4 * K], F32, name="sc4")
+        s_col = const.tile([P, 4], F32, name="s_col")
+        nc.scalar.dma_start(out=s_col[:], in_=Q_scale.rearrange("a b (p t) -> p (a b t)", t=4))
+        q_tiles = []
+        w_sb = const.tile([P, 2, K], BF16, name="w_sb", align_bytes=64)
+        for s in range(LOADS):
+            b, sb = divmod(s, LOADS // BATCH)
+            q_bytes_sb = bytes_pool.tile([P, 4 * K], U8, name="q_bytes_sb")
+            src = Q_bytes[b].rearrange("(s p i) k -> s p (i k)", p=P, i=4)[sb]
+            if s == 0:
+                nc.sync.dma_start(out=q_bytes_sb[:, 0:UW], in_=src[:, 0:UW])
+                nc.sync.dma_start(out=q_bytes_sb[:, UW : 2 * UW], in_=src[:, UW : 2 * UW])
+            else:
+                nc.sync.dma_start(out=q_bytes_sb[:], in_=src)
+            q_tiles.append(q_bytes_sb)
+            if s == 0:
+                nc.sync.dma_start(out=w_sb[:], in_=WQ.rearrange("(r p) k -> p r k", p=P))
+
+        zero = const.tile([P, 1], F32, name="zero")
+        warm = const.tile([P, 1], F32, name="warm")
+        nc.vector.memset(zero[:], 0.0)
+        idle = const.tile([P, K], BF16, name="idle")
+        nc.vector.memset(idle[:], 0.0)
+        nc.scalar.activation(out=warm[:], in_=zero[:], func=ACT.Exp)
+        ident = const.tile([P, P], F32, name="ident")
+        make_identity(nc, ident[:])
+
+        state = {}
+
+        def widen(g):
+            units = GROUPS[g]
+            n = len(units)
+            s, hf = divmod(units[0], 2)
+            xb = xb_pool.tile([P, 2 * UW], BF16, name="xb", align_bytes=64)
+            src = q_tiles[s][:, UW * hf : UW * (hf + n)].bitcast(FP8)
+            if g == 0:
+                for i in range(2):
+                    nc.vector.tensor_tensor(
+                        out=xb[:, K * i : K * (i + 1)],
+                        in0=src[:, K * i : K * (i + 1)],
+                        in1=sc4[:, 0:K],
+                        op=ALU.mult,
+                    )
+            else:
+                nc.vector.tensor_tensor(
+                    out=xb[:, 0 : UW * n], in0=src, in1=sc4[:, 0 : UW * n], op=ALU.mult
+                )
+            state[("xb", g)] = xb[:]
+
+        def turn(g):
+            n = 1 if g < 0 else len(GROUPS[g])
+            words = state[("xb", g)].bitcast(F32)
+            tps = []
+            for a in range(n):
+                tp = tp_pool.tile([P, 2, 2, P], F32, name="tp")
+                for i in range(2):
+                    for u in range(2):
+                        c0 = 512 * a + 256 * i
+                        nc.tensor.transpose(tp[:, i, u, :], words[:, c0 + u : c0 + 256 : 2], ident[:])
+                tps.append(tp)
+            state[("tp", g)] = tps
+
+        def group(g):
+            tps = state[("tp", g)]
+            gt = g_pool.tile([P, 2 * UW], BF16, name="gt", align_bytes=64)
+            for a in range(len(tps)):
+                nc.scalar.copy(
+                    out=gt[:, UW * a : UW * (a + 1)]
+                    .bitcast(F32)
+                    .rearrange("p (i r u) -> p i r u", i=2, u=2),
+                    in_=tps[a][:].rearrange("p i u r -> p i r u"),
+                )
+            state[("g", g)] = gt
+
+        def quantize(g):
+            n = 1 if g < 0 else len(GROUPS[g])
+            gt = state[("g", g)]
+            pool = const if g < 0 else c_pool
+            codes = pool.tile([P, 512], U32, name="w_codes" if g < 0 else "codes", align_bytes=64)
+            scl = pool.tile([P, 512], U8, name="w_scl" if g < 0 else "scl", align_bytes=64)
+            nc.vector.quantize_mx(
+                out=codes[:, 0 : 256 * n].bitcast(FP8X4),
+                scales=scl[:, 0 : 256 * n],
+                in_=gt[:, 0 : UW * n],
+            )
+            state[("c", g)] = (codes, scl)
+
+        def multiply(g):
+            codes, scl = state[("c", g)]
+            w_codes, w_scl = state[("c", -1)]
+            qps = []
+            for a in range(len(GROUPS[g])):
+                qp = qp_pool.tile([P, 2, HEADS * DK], F32, name="qp")
+                for i in range(2):
+                    c0 = 256 * a + P * i
+                    nc.tensor.matmul_mx(
+                        out=qp[:, i, :],
+                        lhsT=codes[:, c0 : c0 + P].bitcast(FP8X4),
+                        lhsT_scale=scl[:, c0 : c0 + P],
+                        rhs=w_codes[:, 0:256].bitcast(FP8X4),
+                        rhs_scale=w_scl[:, 0:256],
+                        start=True,
+                        stop=True,
+                    )
+                qps.append(qp)
+            state[("qp", g)] = qps
+
+        def maxima(g):
+            qps = state[("qp", g)]
+            nm = st_pool.tile([P, 8], F32, name="nm")
+            for a in range(len(qps)):
+                nc.vector.tensor_reduce(
+                    out=nm[:, 4 * a : 4 * (a + 1)],
+                    in_=qps[a][:].rearrange("p i (h d) -> p (i h) d", h=HEADS),
+                    axis=AX.X,
+                    op=ALU.max,
+                    negate=True,
+                )
+            state[("nm", g)] = nm
+
+        def exps(g):
+            qps = state[("qp", g)]
+            nm = state[("nm", g)]
+            sm = st_pool.tile([P, 8], F32, name="sm")
+            es = []
+            for a in range(len(qps)):
+                e = e_pool.tile([P, HEADS, 2, DK], F32, name="e")
+                for i in range(2):
+                    for h in range(HEADS):
+                        c = 4 * a + 2 * i + h
+                        nc.scalar.activation(
+                            out=e[:, h, i, :],
+                            in_=qps[a][:, i, DK * h : DK * (h + 1)],
+                            func=ACT.Exp,
+                            bias=nm[:, c : c + 1],
+                            scale=1.0,
+                            accum_out=sm[:, c : c + 1],
+                        )
+                es.append(e)
+            state[("e", g)] = (es, sm)
+
+        def recip(g):
+            es, sm = state[("e", g)]
+            n = len(es)
+            rs = st_pool.tile([P, 8], F32, name="rs")
+            nc.vector.reciprocal(out=rs[:, 0 : 4 * n], in_=sm[:, 0 : 4 * n])
+            state[("rs", g)] = rs
+            state[("o", g)] = [
+                o_pool.tile([P, HEADS, 2, DK], F32, name="o") for a in range(n)
+            ]
+
+        def normalize(g, engine):
+            es, sm = state[("e", g)]
+            rs = state[("rs", g)]
+            o_tiles = state[("o", g)]
+            tail = g >= n_groups - TAIL_GROUPS
+            for a in range(len(es)):
+                for i in range(2):
+                    for h in range(HEADS):
+                        c = 4 * a + 2 * i + h
+                        if tail and len(es) == 1:
+                            who = "vector" if c % 2 == 1 else "scalar"
+                        elif tail:
+                            who = "vector" if c in TAIL_VECTOR else "scalar"
+                        else:
+                            who = "gpsimd" if c in POOL_SHARE[len(es)] else "scalar"
+                        if who != engine:
+                            continue
+                        dst = o_tiles[a][:, h, i, :]
+                        src = es[a][:, h, i, :]
+                        col = rs[:, c : c + 1]
+                        if who == "scalar":
+                            nc.scalar.activation(out=dst, in_=src, func=ACT.Copy, scale=col)
+                        elif who == "vector":
+                            nc.vector.tensor_scalar(
+                                out=dst, in0=src, scalar1=col, scalar2=None, op0=ALU.mult
+                            )
+                        else:
+                            nc.gpsimd.tensor_scalar(
+                                out=dst, in0=src, scalar1=col, scalar2=0.0, op0=ALU.mult, op1=ALU.add
+                            )
+
+        def store(g):
+            o_tiles = state[("o", g)]
+            for a in range(len(o_tiles)):
+                s, hf = divmod(GROUPS[g][a], 2)
+                b, sb = divmod(s, LOADS // BATCH)
+                dst = out[b].rearrange("h (s p i) d -> s p h (i d)", p=P, i=4)[sb]
+                nc.sync.dma_start(
+                    out=dst[:, :, 2 * DK * hf : 2 * DK * (hf + 1)],
+                    in_=o_tiles[a][:].rearrange("p h i d -> p h (i d)"),
+                )
+
+        junk = tp_pool.tile([P, K], F32, name="tp")
+        for w in range(WARM_MATMULS):
+            nc.tensor.matmul(out=junk[:], lhsT=idle[:, 0:P], rhs=idle[:], start=True, stop=True)
+        scp = tp_pool.tile([P, 4, P], F32, name="tp")
+        for t in range(4):
+            nc.tensor.transpose(scp[:, t, :], s_col[:, t : t + 1].to_broadcast([P, P]), ident[:])
+        nc.scalar.copy(
+            out=sc4[:, 0:K].rearrange("p (n t) -> p n t", t=4),
+            in_=scp[:].rearrange("p t n -> p n t"),
+        )
+        nc.scalar.copy(out=sc4[:, K : 2 * K], in_=sc4[:, 0:K])
+        state[("xb", -1)] = w_sb[:].rearrange("p r k -> p (r k)")
+        turn(-1)
+        group(-1)
+
+        def ok(g):
+            return 0 <= g < n_groups
+
+        for it in range(-1, n_groups + 3):
+            if ok(it + 1):
+                widen(it + 1)
+                turn(it + 1)
+            if ok(it - 3):
+                recip(it - 3)
+                normalize(it - 3, "gpsimd")
+                normalize(it - 3, "scalar")
+            if it == 0:
+                quantize(-1)
+            if ok(it):
+                quantize(it)
+                multiply(it)
+            if ok(it + 1):
+                group(it + 1)
+            if it == 1:
+                nc.scalar.copy(out=sc4[:, 2 * K : 4 * K], in_=sc4[:, 0 : 2 * K])
+            if ok(it - 1):
+                maxima(it - 1)
+                exps(it - 1)
+            if ok(it - 3):
+                normalize(it - 3, "vector")
+                store(it - 3)

@@ -53,7 +53,7 @@ def tile_multiheadattention_pb_t_kernel(tc, Q_bytes, Q_scale, WQ, out):
 
         sc4 = const.tile([P, 4 * K], F32, name="sc4")
         s_col = const.tile([P, 4], F32, name="s_col")
-        nc.scalar.dma_start(out=s_col[:], in_=Q_scale.rearrange("a b (p t) -> p (a b t)", t=4))
+        nc.sync.dma_start(out=s_col[:], in_=Q_scale.rearrange("a b (p t) -> p (a b t)", t=4))
         q_tiles = []
         w_sb = const.tile([P, 2, K], BF16, name="w_sb", align_bytes=64)
         for s in range(LOADS):

@@ -29,7 +29,7 @@ GROUPS = (
     + [[u, u + 1] for u in range(4, UNITS - 2, 2)]
     + [[UNITS - 2], [UNITS - 1]]
 )
-POOL_SHARE = {1: (3,), 2: (0, 5)}
+POOL_SHARE = {1: (3,), 2: (0, 3, 6)}
 TAIL_GROUPS = 5
 TAIL_VECTOR = (1, 2, 4, 5, 7)
 WARM_MATMULS = 4

@@ -25,10 +25,12 @@ UNITS = 32
 UW = 2 * K
 
 GROUPS = (
-    [[u] for u in range(4)]
+    [[u] for u in range(1, 4)]
     + [[u, u + 1] for u in range(4, UNITS - 2, 2)]
-    + [[UNITS - 2], [UNITS - 1]]
+    + [[UNITS - 2], [UNITS - 1], [0]]
 )
+EARLY = len(GROUPS) - 1
+PLANE_STEPS = (5, 7, 9, 11)
 POOL_SHARE = {1: (3,), 2: (0, 3, 6)}
 TAIL_GROUPS = 5
 TAIL_VECTOR = (1, 2, 4, 5, 7)
@@ -79,6 +81,9 @@ def tile_multiheadattention_pb_t_kernel(tc, Q_bytes, Q_scale, WQ, out):
         make_identity(nc, ident[:])
 
         state = {}
+        gx_raw = const.tile([P, UW], BF16, name="gx_raw", align_bytes=64)
+        gx = const.tile([P, UW], BF16, name="gx", align_bytes=64)
+        state[("g", EARLY)] = gx
 
         def widen(g):
             units = GROUPS[g]
@@ -99,6 +104,28 @@ def tile_multiheadattention_pb_t_kernel(tc, Q_bytes, Q_scale, WQ, out):
                     out=xb[:, 0 : UW * n], in0=src, in1=sc4[:, 0 : UW * n], op=ALU.mult
                 )
             state[("xb", g)] = xb[:]
+
+        def cast(g):
+            s, hf = divmod(GROUPS[g][0], 2)
+            xb = xb_pool.tile([P, 2 * UW], BF16, name="xb", align_bytes=64)
+            nc.vector.tensor_copy(
+                out=xb[:, 0:UW], in_=q_tiles[s][:, UW * hf : UW * (hf + 1)].bitcast(FP8)
+            )
+            state[("xb", g)] = xb[:]
+
+        def raw_group(g):
+            nc.scalar.copy(
+                out=gx_raw[:].bitcast(F32).rearrange("p (i r u) -> p i r u", i=2, u=2),
+                in_=state[("tp", g)][0][:].rearrange("p i u r -> p i r u"),
+            )
+
+        def plane(t):
+            nc.scalar.activation(
+                out=gx[:].rearrange("p (c t) -> p c t", t=4)[:, :, t],
+                in_=gx_raw[:].rearrange("p (c t) -> p c t", t=4)[:, :, t],
+                func=ACT.Copy,
+                scale=s_col[:, t : t + 1],
+            )
 
         def turn(g):
             n = 1 if g < 0 else len(GROUPS[g])
@@ -255,6 +282,9 @@ def tile_multiheadattention_pb_t_kernel(tc, Q_bytes, Q_scale, WQ, out):
             in_=scp[:].rearrange("p t n -> p n t"),
         )
         nc.scalar.copy(out=sc4[:, K : 2 * K], in_=sc4[:, 0:K])
+        cast(EARLY)
+        turn(EARLY)
+        raw_group(EARLY)
         state[("xb", -1)] = w_sb[:].rearrange("p r k -> p (r k)")
         turn(-1)
         group(-1)
@@ -263,21 +293,23 @@ def tile_multiheadattention_pb_t_kernel(tc, Q_bytes, Q_scale, WQ, out):
             return 0 <= g < n_groups
 
         for it in range(-1, n_groups + 3):
-            if ok(it + 1):
+            if ok(it + 1) and it + 1 != EARLY:
                 widen(it + 1)
                 turn(it + 1)
             if ok(it - 3):
                 recip(it - 3)
                 normalize(it - 3, "gpsimd")
                 normalize(it - 3, "scalar")
+            if it in PLANE_STEPS:
+                plane(PLANE_STEPS.index(it))
             if it == 0:
                 quantize(-1)
             if ok(it):
                 quantize(it)
                 multiply(it)
-            if ok(it + 1):
+            if ok(it + 1) and it + 1 != EARLY:
                 group(it + 1)
-            if it == 1:
+            if it == 0:
                 nc.scalar.copy(out=sc4[:, 2 * K : 4 * K], in_=sc4[:, 0 : 2 * K])
             if ok(it - 1):
                 maxima(it - 1)

@@ -25,14 +25,14 @@ UNITS = 32
 UW = 2 * K
 
 GROUPS = (
-    [[u] for u in range(1, 4)]
-    + [[u, u + 1] for u in range(4, UNITS - 2, 2)]
-    + [[UNITS - 2], [UNITS - 1], [0]]
+    [[u] for u in range(2, 6)]
+    + [[u, u + 1] for u in range(6, UNITS - 2, 2)]
+    + [[UNITS - 2], [UNITS - 1], [0], [1]]
 )
-EARLY = len(GROUPS) - 1
-PLANE_STEPS = (5, 7, 9, 11)
+EARLY = (len(GROUPS) - 2, len(GROUPS) - 1)
+PLANE_STEPS = (4, 5, 6, 7, 8, 9, 10, 11)
 POOL_SHARE = {1: (3,), 2: (0, 3, 6)}
-TAIL_GROUPS = 5
+TAIL_GROUPS = 6
 TAIL_VECTOR = (1, 2, 4, 5, 7)
 WARM_MATMULS = 4
 
@@ -81,9 +81,10 @@ def tile_multiheadattention_pb_t_kernel(tc, Q_bytes, Q_scale, WQ, out):
         make_identity(nc, ident[:])
 
         state = {}
-        gx_raw = const.tile([P, UW], BF16, name="gx_raw", align_bytes=64)
-        gx = const.tile([P, UW], BF16, name="gx", align_bytes=64)
-        state[("g", EARLY)] = gx
+        gx_raw = {}
+        for x in range(2):
+            gx_raw[EARLY[x]] = const.tile([P, UW], BF16, name="gx_raw%d" % x, align_bytes=64)
+            state[("g", EARLY[x])] = const.tile([P, UW], BF16, name="gx%d" % x, align_bytes=64)
 
         def widen(g):
             units = GROUPS[g]
@@ -115,14 +116,14 @@ def tile_multiheadattention_pb_t_kernel(tc, Q_bytes, Q_scale, WQ, out):
 
         def raw_group(g):
             nc.scalar.copy(
-                out=gx_raw[:].bitcast(F32).rearrange("p (i r u) -> p i r u", i=2, u=2),
+                out=gx_raw[g][:].bitcast(F32).rearrange("p (i r u) -> p i r u", i=2, u=2),
                 in_=state[("tp", g)][0][:].rearrange("p i u r -> p i r u"),
             )
 
-        def plane(t):
+        def plane(g, t):
             nc.scalar.activation(
-                out=gx[:].rearrange("p (c t) -> p c t", t=4)[:, :, t],
-                in_=gx_raw[:].rearrange("p (c t) -> p c t", t=4)[:, :, t],
+                out=state[("g", g)][:].rearrange("p (c t) -> p c t", t=4)[:, :, t],
+                in_=gx_raw[g][:].rearrange("p (c t) -> p c t", t=4)[:, :, t],
                 func=ACT.Copy,
                 scale=s_col[:, t : t + 1],
             )
@@ -282,9 +283,11 @@ def tile_multiheadattention_pb_t_kernel(tc, Q_bytes, Q_scale, WQ, out):
             in_=scp[:].rearrange("p t n -> p n t"),
         )
         nc.scalar.copy(out=sc4[:, K : 2 * K], in_=sc4[:, 0:K])
-        cast(EARLY)
-        turn(EARLY)
-        raw_group(EARLY)
+        cast(EARLY[0])
+        turn(EARLY[0])
+        raw_group(EARLY[0])
+        cast(EARLY[1])
+        turn(EARLY[1])
         state[("xb", -1)] = w_sb[:].rearrange("p r k -> p (r k)")
         turn(-1)
         group(-1)
@@ -293,7 +296,7 @@ def tile_multiheadattention_pb_t_kernel(tc, Q_bytes, Q_scale, WQ, out):
             return 0 <= g < n_groups
 
         for it in range(-1, n_groups + 3):
-            if ok(it + 1) and it + 1 != EARLY:
+            if ok(it + 1) and it + 1 not in EARLY:
                 widen(it + 1)
                 turn(it + 1)
             if ok(it - 3):
@@ -301,15 +304,17 @@ def tile_multiheadattention_pb_t_kernel(tc, Q_bytes, Q_scale, WQ, out):
                 normalize(it - 3, "gpsimd")
                 normalize(it - 3, "scalar")
             if it in PLANE_STEPS:
-                plane(PLANE_STEPS.index(it))
+                plane(EARLY[PLANE_STEPS.index(it) // 4], PLANE_STEPS.index(it) % 4)
             if it == 0:
                 quantize(-1)
             if ok(it):
                 quantize(it)
                 multiply(it)
-            if ok(it + 1) and it + 1 != EARLY:
+            if ok(it + 1) and it + 1 not in EARLY:
                 group(it + 1)
-            if it == 0:
+            if it == -1:
+                raw_group(EARLY[1])
+            if it == 1:
                 nc.scalar.copy(out=sc4[:, 2 * K : 4 * K], in_=sc4[:, 0 : 2 * K])
             if ok(it - 1):
                 maxima(it - 1)

@@ -25,14 +25,14 @@ UNITS = 32
 UW = 2 * K
 
 GROUPS = (
-    [[u] for u in range(2, 6)]
+    [[u] for u in range(3, 6)]
     + [[u, u + 1] for u in range(6, UNITS - 2, 2)]
-    + [[UNITS - 2], [UNITS - 1], [0], [1]]
+    + [[UNITS - 2], [UNITS - 1], [0], [1], [2]]
 )
-EARLY = (len(GROUPS) - 2, len(GROUPS) - 1)
-PLANE_STEPS = (4, 5, 6, 7, 8, 9, 10, 11)
-POOL_SHARE = {1: (3,), 2: (0, 3, 6)}
-TAIL_GROUPS = 6
+EARLY = (len(GROUPS) - 3, len(GROUPS) - 2, len(GROUPS) - 1)
+WEAVE_STEPS = (4, 5, 6, 7, 8, 9)
+POOL_SHARE = {1: (3,), 2: (0, 2, 4, 6)}
+TAIL_GROUPS = 7
 TAIL_VECTOR = (1, 2, 4, 5, 7)
 WARM_MATMULS = 4
 
@@ -62,14 +62,14 @@ def tile_multiheadattention_pb_t_kernel(tc, Q_bytes, Q_scale, WQ, out):
             b, sb = divmod(s, LOADS // BATCH)
             q_bytes_sb = bytes_pool.tile([P, 4 * K], U8, name="q_bytes_sb")
             src = Q_bytes[b].rearrange("(s p i) k -> s p (i k)", p=P, i=4)[sb]
-            if s == 0:
+            if s <= 1:
                 nc.sync.dma_start(out=q_bytes_sb[:, 0:UW], in_=src[:, 0:UW])
+                if s == 1:
+                    nc.sync.dma_start(out=w_sb[:], in_=WQ.rearrange("(r p) k -> p r k", p=P))
                 nc.sync.dma_start(out=q_bytes_sb[:, UW : 2 * UW], in_=src[:, UW : 2 * UW])
             else:
                 nc.sync.dma_start(out=q_bytes_sb[:], in_=src)
             q_tiles.append(q_bytes_sb)
-            if s == 0:
-                nc.sync.dma_start(out=w_sb[:], in_=WQ.rearrange("(r p) k -> p r k", p=P))
 
         zero = const.tile([P, 1], F32, name="zero")
         warm = const.tile([P, 1], F32, name="warm")
@@ -82,8 +82,8 @@ def tile_multiheadattention_pb_t_kernel(tc, Q_bytes, Q_scale, WQ, out):
 
         state = {}
         gx_raw = {}
-        for x in range(2):
-            gx_raw[EARLY[x]] = const.tile([P, UW], BF16, name="gx_raw%d" % x, align_bytes=64)
+        for x in range(3):
+            gx_raw[EARLY[x]] = const.tile([P, 4, 2 * P], BF16, name="gx_raw%d" % x, align_bytes=64)
             state[("g", EARLY[x])] = const.tile([P, UW], BF16, name="gx%d" % x, align_bytes=64)
 
         def widen(g):
@@ -114,18 +114,20 @@ def tile_multiheadattention_pb_t_kernel(tc, Q_bytes, Q_scale, WQ, out):
             )
             state[("xb", g)] = xb[:]
 
-        def raw_group(g):
-            nc.scalar.copy(
-                out=gx_raw[g][:].bitcast(F32).rearrange("p (i r u) -> p i r u", i=2, u=2),
-                in_=state[("tp", g)][0][:].rearrange("p i u r -> p i r u"),
-            )
-
         def plane(g, t):
+            u, e = divmod(t, 2)
+            src = state[("tp", g)][0][:].bitcast(BF16)[:, :, u, :]
             nc.scalar.activation(
-                out=state[("g", g)][:].rearrange("p (c t) -> p c t", t=4)[:, :, t],
-                in_=gx_raw[g][:].rearrange("p (c t) -> p c t", t=4)[:, :, t],
+                out=gx_raw[g][:, t, :].rearrange("p (i r) -> p i r", i=2),
+                in_=src.rearrange("p i (r e) -> p i r e", e=2)[:, :, :, e],
                 func=ACT.Copy,
                 scale=s_col[:, t : t + 1],
+            )
+
+        def weave(g, half):
+            nc.scalar.copy(
+                out=state[("g", g)][:, K * half : K * (half + 1)].rearrange("p (c t) -> p c t", t=4),
+                in_=gx_raw[g][:, :, P * half : P * (half + 1)].rearrange("p t c -> p c t"),
             )
 
         def turn(g):
@@ -133,7 +135,10 @@ def tile_multiheadattention_pb_t_kernel(tc, Q_bytes, Q_scale, WQ, out):
             words = state[("xb", g)].bitcast(F32)
             tps = []
             for a in range(n):
-                tp = tp_pool.tile([P, 2, 2, P], F32, name="tp")
+                if g in EARLY:
+                    tp = qp_pool.tile([P, 2, 2, P], F32, name="qp")
+                else:
+                    tp = tp_pool.tile([P, 2, 2, P], F32, name="tp")
                 for i in range(2):
                     for u in range(2):
                         c0 = 512 * a + 256 * i
@@ -285,12 +290,15 @@ def tile_multiheadattention_pb_t_kernel(tc, Q_bytes, Q_scale, WQ, out):
         nc.scalar.copy(out=sc4[:, K : 2 * K], in_=sc4[:, 0:K])
         cast(EARLY[0])
         turn(EARLY[0])
-        raw_group(EARLY[0])
+        for t in range(4):
+            plane(EARLY[0], t)
         cast(EARLY[1])
         turn(EARLY[1])
         state[("xb", -1)] = w_sb[:].rearrange("p r k -> p (r k)")
         turn(-1)
         group(-1)
+        cast(EARLY[2])
+        turn(EARLY[2])
 
         def ok(g):
             return 0 <= g < n_groups
@@ -303,8 +311,8 @@ def tile_multiheadattention_pb_t_kernel(tc, Q_bytes, Q_scale, WQ, out):
                 recip(it - 3)
                 normalize(it - 3, "gpsimd")
                 normalize(it - 3, "scalar")
-            if it in PLANE_STEPS:
-                plane(EARLY[PLANE_STEPS.index(it) // 4], PLANE_STEPS.index(it) % 4)
+            if it in WEAVE_STEPS:
+                weave(EARLY[WEAVE_STEPS.index(it) // 2], WEAVE_STEPS.index(it) % 2)
             if it == 0:
                 quantize(-1)
             if ok(it):
@@ -312,13 +320,17 @@ def tile_multiheadattention_pb_t_kernel(tc, Q_bytes, Q_scale, WQ, out):
                 multiply(it)
             if ok(it + 1) and it + 1 not in EARLY:
                 group(it + 1)
-            if it == -1:
-                raw_group(EARLY[1])
-            if it == 1:
+            if it == 0:
                 nc.scalar.copy(out=sc4[:, 2 * K : 4 * K], in_=sc4[:, 0 : 2 * K])
+            if it in (-1, 0):
+                plane(EARLY[1], 2 * it + 2)
+                plane(EARLY[1], 2 * it + 3)
             if ok(it - 1):
                 maxima(it - 1)
                 exps(it - 1)
+            if it == 1:
+                for t in range(4):
+                    plane(EARLY[2], t)
             if ok(it - 3):
                 normalize(it - 3, "vector")
                 store(it - 3)

@@ -31,7 +31,7 @@ GROUPS = (
 )
 EARLY = (len(GROUPS) - 3, len(GROUPS) - 2, len(GROUPS) - 1)
 WEAVE_STEPS = (4, 5, 6, 7, 8, 9)
-POOL_SHARE = {1: (3,), 2: (0, 2, 4, 6)}
+POOL_SHARE = {1: (3,), 2: (0, 3, 6)}
 TAIL_GROUPS = 7
 TAIL_VECTOR = (1, 2, 4, 5, 7)
 WARM_MATMULS = 4

@@ -245,7 +245,7 @@ def tile_multiheadattention_pb_t_kernel(tc, Q_bytes, Q_scale, WQ, out):
                     for h in range(HEADS):
                         c = 4 * a + 2 * i + h
                         if tail and len(es) == 1:
-                            who = "vector" if c % 2 == 1 else "scalar"
+                            who = "vector" if c > 0 else "scalar"
                         elif tail:
                             who = "vector" if c in TAIL_VECTOR else "scalar"
                         else:

@@ -245,9 +245,9 @@ def tile_multiheadattention_pb_t_kernel(tc, Q_bytes, Q_scale, WQ, out):
                     for h in range(HEADS):
                         c = 4 * a + 2 * i + h
                         if tail and len(es) == 1:
-                            who = "vector" if c > 0 else "scalar"
+                            who = "gpsimd" if c == 3 else ("vector" if c > 0 else "scalar")
                         elif tail:
-                            who = "vector" if c in TAIL_VECTOR else "scalar"
+                            who = "gpsimd" if c in POOL_SHARE[2] else ("vector" if c in TAIL_VECTOR else "scalar")
                         else:
                             who = "gpsimd" if c in POOL_SHARE[len(es)] else "scalar"
                         if who != engine:

from contextlib import ExitStack

import concourse.mybir as mybir
from concourse.masks import make_identity

FLOPS = 2 * 8192 * 512 * 256

F32 = mybir.dt.float32
BF16 = mybir.dt.bfloat16
U32 = mybir.dt.uint32
U8 = mybir.dt.uint8
FP8 = mybir.dt.float8_e4m3fn
FP8X4 = mybir.dt.float8_e4m3fn_x4
ACT = mybir.ActivationFunctionType
ALU = mybir.AluOpType
AX = mybir.AxisListType

P = 128
K = 512
BATCH = 4
HEADS = 2
DK = 128
LOADS = 16
UNITS = 32
UW = 2 * K

GROUPS = (
    [[u] for u in range(3, 6)]
    + [[u, u + 1] for u in range(6, UNITS - 2, 2)]
    + [[UNITS - 2], [UNITS - 1], [0], [1], [2]]
)
EARLY = (len(GROUPS) - 3, len(GROUPS) - 2, len(GROUPS) - 1)
WEAVE_STEPS = (4, 5, 6, 7, 8, 9)
POOL_SHARE = {1: (3,), 2: (0, 3, 6)}
TAIL_GROUPS = 7
TAIL_VECTOR = (1, 2, 4, 5, 7)
WARM_MATMULS = 4


def tile_multiheadattention_pb_t_kernel(tc, Q_bytes, Q_scale, WQ, out):
    nc = tc.nc
    n_groups = len(GROUPS)
    with ExitStack() as ctx:
        const = ctx.enter_context(tc.tile_pool(name="const", bufs=1))
        bytes_pool = ctx.enter_context(tc.tile_pool(name="bytes_pool", bufs=LOADS))
        xb_pool = ctx.enter_context(tc.tile_pool(name="xb_pool", bufs=3))
        g_pool = ctx.enter_context(tc.tile_pool(name="g_pool", bufs=3))
        c_pool = ctx.enter_context(tc.tile_pool(name="c_pool", bufs=3))
        st_pool = ctx.enter_context(tc.tile_pool(name="st_pool", bufs=5))
        e_pool = ctx.enter_context(tc.tile_pool(name="e_pool", bufs=8))
        o_pool = ctx.enter_context(tc.tile_pool(name="o_pool", bufs=8))
        tp_pool = ctx.enter_context(tc.psum_pool(name="tp_pool", bufs=4))
        qp_pool = ctx.enter_context(tc.psum_pool(name="qp_pool", bufs=4))
        ctx.enter_context(tc.manual_schedule())

        sc4 = const.tile([P, 4 * K], F32, name="sc4")
        s_col = const.tile([P, 4], F32, name="s_col")
        nc.sync.dma_start(out=s_col[:], in_=Q_scale.rearrange("a b (p t) -> p (a b t)", t=4))
        q_tiles = []
        w_sb = const.tile([P, 2, K], BF16, name="w_sb", align_bytes=64)
        for s in range(LOADS):
            b, sb = divmod(s, LOADS // BATCH)
            q_bytes_sb = bytes_pool.tile([P, 4 * K], U8, name="q_bytes_sb")
            src = Q_bytes[b].rearrange("(s p i) k -> s p (i k)", p=P, i=4)[sb]
            if s <= 1:
                nc.sync.dma_start(out=q_bytes_sb[:, 0:UW], in_=src[:, 0:UW])
                if s == 1:
                    nc.sync.dma_start(out=w_sb[:], in_=WQ.rearrange("(r p) k -> p r k", p=P))
                nc.sync.dma_start(out=q_bytes_sb[:, UW : 2 * UW], in_=src[:, UW : 2 * UW])
            else:
                nc.sync.dma_start(out=q_bytes_sb[:], in_=src)
            q_tiles.append(q_bytes_sb)

        zero = const.tile([P, 1], F32, name="zero")
        warm = const.tile([P, 1], F32, name="warm")
        nc.vector.memset(zero[:], 0.0)
        idle = const.tile([P, K], BF16, name="idle")
        nc.vector.memset(idle[:], 0.0)
        nc.scalar.activation(out=warm[:], in_=zero[:], func=ACT.Exp)
        ident = const.tile([P, P], F32, name="ident")
        make_identity(nc, ident[:])

        state = {}
        gx_raw = {}
        for x in range(3):
            gx_raw[EARLY[x]] = const.tile([P, 4, 2 * P], BF16, name="gx_raw%d" % x, align_bytes=64)
            state[("g", EARLY[x])] = const.tile([P, UW], BF16, name="gx%d" % x, align_bytes=64)

        def widen(g):
            units = GROUPS[g]
            n = len(units)
            s, hf = divmod(units[0], 2)
            xb = xb_pool.tile([P, 2 * UW], BF16, name="xb", align_bytes=64)
            src = q_tiles[s][:, UW * hf : UW * (hf + n)].bitcast(FP8)
            if g == 0:
                for i in range(2):
                    nc.vector.tensor_tensor(
                        out=xb[:, K * i : K * (i + 1)],
                        in0=src[:, K * i : K * (i + 1)],
                        in1=sc4[:, 0:K],
                        op=ALU.mult,
                    )
            else:
                nc.vector.tensor_tensor(
                    out=xb[:, 0 : UW * n], in0=src, in1=sc4[:, 0 : UW * n], op=ALU.mult
                )
            state[("xb", g)] = xb[:]

        def cast(g):
            s, hf = divmod(GROUPS[g][0], 2)
            xb = xb_pool.tile([P, 2 * UW], BF16, name="xb", align_bytes=64)
            nc.vector.tensor_copy(
                out=xb[:, 0:UW], in_=q_tiles[s][:, UW * hf : UW * (hf + 1)].bitcast(FP8)
            )
            state[("xb", g)] = xb[:]

        def plane(g, t):
            u, e = divmod(t, 2)
            src = state[("tp", g)][0][:].bitcast(BF16)[:, :, u, :]
            nc.scalar.activation(
                out=gx_raw[g][:, t, :].rearrange("p (i r) -> p i r", i=2),
                in_=src.rearrange("p i (r e) -> p i r e", e=2)[:, :, :, e],
                func=ACT.Copy,
                scale=s_col[:, t : t + 1],
            )

        def weave(g, half):
            nc.scalar.copy(
                out=state[("g", g)][:, K * half : K * (half + 1)].rearrange("p (c t) -> p c t", t=4),
                in_=gx_raw[g][:, :, P * half : P * (half + 1)].rearrange("p t c -> p c t"),
            )

        def turn(g):
            n = 1 if g < 0 else len(GROUPS[g])
            words = state[("xb", g)].bitcast(F32)
            tps = []
            for a in range(n):
                if g in EARLY:
                    tp = qp_pool.tile([P, 2, 2, P], F32, name="qp")
                else:
                    tp = tp_pool.tile([P, 2, 2, P], F32, name="tp")
                for i in range(2):
                    for u in range(2):
                        c0 = 512 * a + 256 * i
                        nc.tensor.transpose(tp[:, i, u, :], words[:, c0 + u : c0 + 256 : 2], ident[:])
                tps.append(tp)
            state[("tp", g)] = tps

        def group(g):
            tps = state[("tp", g)]
            gt = g_pool.tile([P, 2 * UW], BF16, name="gt", align_bytes=64)
            for a in range(len(tps)):
                nc.scalar.copy(
                    out=gt[:, UW * a : UW * (a + 1)]
                    .bitcast(F32)
                    .rearrange("p (i r u) -> p i r u", i=2, u=2),
                    in_=tps[a][:].rearrange("p i u r -> p i r u"),
                )
            state[("g", g)] = gt

        def quantize(g):
            n = 1 if g < 0 else len(GROUPS[g])
            gt = state[("g", g)]
            pool = const if g < 0 else c_pool
            codes = pool.tile([P, 512], U32, name="w_codes" if g < 0 else "codes", align_bytes=64)
            scl = pool.tile([P, 512], U8, name="w_scl" if g < 0 else "scl", align_bytes=64)
            nc.vector.quantize_mx(
                out=codes[:, 0 : 256 * n].bitcast(FP8X4),
                scales=scl[:, 0 : 256 * n],
                in_=gt[:, 0 : UW * n],
            )
            state[("c", g)] = (codes, scl)

        def multiply(g):
            codes, scl = state[("c", g)]
            w_codes, w_scl = state[("c", -1)]
            qps = []
            for a in range(len(GROUPS[g])):
                qp = qp_pool.tile([P, 2, HEADS * DK], F32, name="qp")
                for i in range(2):
                    c0 = 256 * a + P * i
                    nc.tensor.matmul_mx(
                        out=qp[:, i, :],
                        lhsT=codes[:, c0 : c0 + P].bitcast(FP8X4),
                        lhsT_scale=scl[:, c0 : c0 + P],
                        rhs=w_codes[:, 0:256].bitcast(FP8X4),
                        rhs_scale=w_scl[:, 0:256],
                        start=True,
                        stop=True,
                    )
                qps.append(qp)
            state[("qp", g)] = qps

        def maxima(g):
            qps = state[("qp", g)]
            nm = st_pool.tile([P, 8], F32, name="nm")
            for a in range(len(qps)):
                nc.vector.tensor_reduce(
                    out=nm[:, 4 * a : 4 * (a + 1)],
                    in_=qps[a][:].rearrange("p i (h d) -> p (i h) d", h=HEADS),
                    axis=AX.X,
                    op=ALU.max,
                    negate=True,
                )
            state[("nm", g)] = nm

        def exps(g):
            qps = state[("qp", g)]
            nm = state[("nm", g)]
            sm = st_pool.tile([P, 8], F32, name="sm")
            es = []
            for a in range(len(qps)):
                e = e_pool.tile([P, HEADS, 2, DK], F32, name="e")
                for i in range(2):
                    for h in range(HEADS):
                        c = 4 * a + 2 * i + h
                        nc.scalar.activation(
                            out=e[:, h, i, :],
                            in_=qps[a][:, i, DK * h : DK * (h + 1)],
                            func=ACT.Exp,
                            bias=nm[:, c : c + 1],
                            scale=1.0,
                            accum_out=sm[:, c : c + 1],
                        )
                es.append(e)
            state[("e", g)] = (es, sm)

        def recip(g):
            es, sm = state[("e", g)]
            n = len(es)
            rs = st_pool.tile([P, 8], F32, name="rs")
            nc.vector.reciprocal(out=rs[:, 0 : 4 * n], in_=sm[:, 0 : 4 * n])
            state[("rs", g)] = rs
            state[("o", g)] = [
                o_pool.tile([P, HEADS, 2, DK], F32, name="o") for a in range(n)
            ]

        def normalize(g, engine):
            es, sm = state[("e", g)]
            rs = state[("rs", g)]
            o_tiles = state[("o", g)]
            tail = g >= n_groups - TAIL_GROUPS
            for a in range(len(es)):
                for i in range(2):
                    for h in range(HEADS):
                        c = 4 * a + 2 * i + h
                        if tail and len(es) == 1:
                            who = "gpsimd" if c == 3 else ("vector" if c > 0 else "scalar")
                        elif tail:
                            who = "gpsimd" if c in POOL_SHARE[2] else ("vector" if c in TAIL_VECTOR else "scalar")
                        else:
                            who = "gpsimd" if c in POOL_SHARE[len(es)] else "scalar"
                        if who != engine:
                            continue
                        dst = o_tiles[a][:, h, i, :]
                        src = es[a][:, h, i, :]
                        col = rs[:, c : c + 1]
                        if who == "scalar":
                            nc.scalar.activation(out=dst, in_=src, func=ACT.Copy, scale=col)
                        elif who == "vector":
                            nc.vector.tensor_scalar(
                                out=dst, in0=src, scalar1=col, scalar2=None, op0=ALU.mult
                            )
                        else:
                            nc.gpsimd.tensor_scalar(
                                out=dst, in0=src, scalar1=col, scalar2=0.0, op0=ALU.mult, op1=ALU.add
                            )

        def store(g):
            o_tiles = state[("o", g)]
            for a in range(len(o_tiles)):
                s, hf = divmod(GROUPS[g][a], 2)
                b, sb = divmod(s, LOADS // BATCH)
                dst = out[b].rearrange("h (s p i) d -> s p h (i d)", p=P, i=4)[sb]
                nc.sync.dma_start(
                    out=dst[:, :, 2 * DK * hf : 2 * DK * (hf + 1)],
                    in_=o_tiles[a][:].rearrange("p h i d -> p h (i d)"),
                )

        junk = tp_pool.tile([P, K], F32, name="tp")
        for w in range(WARM_MATMULS):
            nc.tensor.matmul(out=junk[:], lhsT=idle[:, 0:P], rhs=idle[:], start=True, stop=True)
        scp = tp_pool.tile([P, 4, P], F32, name="tp")
        for t in range(4):
            nc.tensor.transpose(scp[:, t, :], s_col[:, t : t + 1].to_broadcast([P, P]), ident[:])
        nc.scalar.copy(
            out=sc4[:, 0:K].rearrange("p (n t) -> p n t", t=4),
            in_=scp[:].rearrange("p t n -> p n t"),
        )
        nc.scalar.copy(out=sc4[:, K : 2 * K], in_=sc4[:, 0:K])
        cast(EARLY[0])
        turn(EARLY[0])
        for t in range(4):
            plane(EARLY[0], t)
        cast(EARLY[1])
        turn(EARLY[1])
        state[("xb", -1)] = w_sb[:].rearrange("p r k -> p (r k)")
        turn(-1)
        group(-1)
        cast(EARLY[2])
        turn(EARLY[2])

        def ok(g):
            return 0 <= g < n_groups

        for it in range(-1, n_groups + 3):
            if ok(it + 1) and it + 1 not in EARLY:
                widen(it + 1)
                turn(it + 1)
            if ok(it - 3):
                recip(it - 3)
                normalize(it - 3, "gpsimd")
                normalize(it - 3, "scalar")
            if it in WEAVE_STEPS:
                weave(EARLY[WEAVE_STEPS.index(it) // 2], WEAVE_STEPS.index(it) % 2)
            if it == 0:
                quantize(-1)
            if ok(it):
                quantize(it)
                multiply(it)
            if ok(it + 1) and it + 1 not in EARLY:
                group(it + 1)
            if it == 0:
                nc.scalar.copy(out=sc4[:, 2 * K : 4 * K], in_=sc4[:, 0 : 2 * K])
            if it in (-1, 0):
                plane(EARLY[1], 2 * it + 2)
                plane(EARLY[1], 2 * it + 3)
            if ok(it - 1):
                maxima(it - 1)
                exps(it - 1)
            if it == 1:
                for t in range(4):
                    plane(EARLY[2], t)
            if ok(it - 3):
                normalize(it - 3, "vector")
                store(it - 3)
